import numpy as np
import ml_dtypes


def mxq(x, axis, fmt="e4m3"):
    dtype, down = {"e4m3": (ml_dtypes.float8_e4m3fn, 7), "e5m2": (ml_dtypes.float8_e5m2, 14)}[fmt]
    v = np.moveaxis(np.asarray(x, np.float32).astype(ml_dtypes.bfloat16).astype(np.float64), axis, -1)
    blocks = v.reshape(v.shape[:-1] + (-1, 32))
    amax = np.abs(blocks).max(-1, keepdims=True)
    byte = np.maximum(np.where(amax > 0, np.frexp(amax)[1] - 1 + 127, 0) - down, 1)
    scale = np.exp2(byte - 127.0)
    codes = (blocks / scale).astype(np.float32).astype(dtype).astype(np.float64)
    return np.moveaxis((codes * scale).reshape(v.shape), -1, axis)


WIDE = False


def mx_kscale(k):
    if not WIDE:
        return np.ones(k)
    levels = np.array([10, -10, 5, -5, 0])
    a = np.random.permutation(np.resize(levels, k // 512 * 4)).reshape(k // 512, 4)
    idx = np.arange(k)
    return np.exp2(a[idx // 512, idx % 128 // 32])


BF16 = ml_dtypes.bfloat16


def bf(x):
    return np.asarray(x, np.float32).astype(BF16)


def f64(x):
    return np.asarray(x).astype(np.float64)


E2M1 = np.array([0.0, 0.5, 1.0, 1.5, 2.0, 3.0, 4.0, 6.0, -0.0, -0.5, -1.0, -1.5, -2.0, -3.0, -4.0, -6.0])


def pack_weight(w, fmt):
    k, n = w.shape
    w = f64(bf(w)).reshape(k // 32, 32, n)
    amax = np.abs(w).max(1)
    if fmt == "e4m3":
        byte = np.frexp(amax)[1] - 1 + 127 - 7
    else:
        mant, ex = np.frexp(amax / 6.0)
        byte = np.where(mant > 0.5, ex, ex - 1) + 127
    byte = np.clip(np.where(amax > 0, byte, 1), 1, 254)
    scaled = (w * np.exp2(127.0 - byte)[:, None, :]).reshape(k, n).astype(np.float32)
    by_word = np.ascontiguousarray(scaled.reshape(k // 512, 128, 4, n).transpose(0, 1, 3, 2))
    if fmt == "e4m3":
        words = by_word.astype(ml_dtypes.float8_e4m3fn).view(np.uint8)
    else:
        c = by_word.astype(ml_dtypes.float4_e2m1fn).view(np.uint8) & 0xF
        words = c[..., 0::2] | (c[..., 1::2] << 4)
    return np.ascontiguousarray(words), np.ascontiguousarray(byte.astype(np.uint8).reshape(k // 512, 16, n))


def unpack_weight(words, scales, fmt):
    g, p, n, _ = words.shape
    if fmt == "e4m3":
        vals = np.ascontiguousarray(words).view(ml_dtypes.float8_e4m3fn).astype(np.float64)
    else:
        nib = np.empty((g, p, n, 4), np.uint8)
        nib[..., 0::2] = words & 0xF
        nib[..., 1::2] = words >> 4
        vals = E2M1[nib]
    vals = vals * np.repeat(np.exp2(scales.astype(np.float64) - 127.0), 8, axis=1)[..., None]
    return vals.transpose(0, 1, 3, 2).reshape(g * 512, n)

def pack4(w):
    words, scales = pack_weight(w, "e2m1")
    return words.reshape(words.shape[0], 128, -1), scales


def unpack4(words, scales):
    return unpack_weight(words.reshape(words.shape[0], 128, -1, 2), scales, "e2m1")


B, D, H = 256, 1024, 2048
M_SCALE = 1.5


def setup_inputs():
    s, t = mx_kscale(D), mx_kscale(H)
    x = bf(np.random.standard_normal((B, D)) * s)
    h_prev = bf(np.random.standard_normal((B, H)) * t)
    c_prev = bf(np.random.standard_normal((B, H)))
    W_ih = np.random.standard_normal((2 * H, D)) * 0.7 / np.sqrt(D) / s[None, :]
    b_ih = bf(np.random.standard_normal(2 * H) * 0.2)
    W_hh = np.random.standard_normal((2 * H, H)) * 0.7 / np.sqrt(H) / t[None, :]
    b_hh = bf(np.random.standard_normal(2 * H) * 0.2)
    log_lambda = bf(np.log(np.random.uniform(0.05, 0.5, H)))
    z_bias = bf(np.random.standard_normal(H) * 0.2)
    m_bias = bf(np.random.standard_normal(H) * 0.2)
    W_ih_words, W_ih_scales = pack4(np.ascontiguousarray(W_ih.T))
    W_hh_words, W_hh_scales = pack4(np.ascontiguousarray(W_hh.T))
    return {'x': x,
            'h_prev': h_prev,
            'c_prev': c_prev,
            'W_ih_words': W_ih_words,
            'W_ih_scales': W_ih_scales,
            'b_ih': b_ih,
            'W_hh_words': W_hh_words,
            'W_hh_scales': W_hh_scales,
            'b_hh': b_hh,
            'log_lambda': log_lambda,
            'z_bias': z_bias,
            'm_bias': m_bias}


def reference(x, h_prev, c_prev, W_ih_words, W_ih_scales, b_ih, W_hh_words, W_hh_scales, b_hh, log_lambda, z_bias, m_bias):
    gates = ((mxq(f64(x), 1, 'e4m3') @ unpack4(W_ih_words, W_ih_scales)) + f64(b_ih)
             + (mxq(f64(h_prev), 1, 'e4m3') @ unpack4(W_hh_words, W_hh_scales)) + f64(b_hh))
    z_raw, m_raw = gates[:, :H], gates[:, H:]
    z_t = np.tanh(z_raw + f64(z_bias))
    M_t = M_SCALE * np.tanh(m_raw + f64(m_bias))
    A_base = -np.exp(f64(log_lambda))
    innov = z_t - M_t * (A_base * f64(c_prev))
    return z_t, M_t, innov

@@ -1,0 +1,173 @@
+from contextlib import ExitStack
+
+import concourse.mybir as mybir
+from concourse.masks import make_identity
+
+F32 = mybir.dt.float32
+BF16 = mybir.dt.bfloat16
+I32 = mybir.dt.int32
+U32 = mybir.dt.uint32
+U8 = mybir.dt.uint8
+FP8X4 = mybir.dt.float8_e4m3fn_x4
+FP4X4 = mybir.dt.float4_e2m1fn_x4
+ACT = mybir.ActivationFunctionType
+
+P = 128
+K_PASS = 512
+BATCH, D_IN, HID = 256, 1024, 2048
+GATES = 2 * HID
+K_ALL = D_IN + HID
+PASSES = K_ALL // K_PASS
+X_PASSES = D_IN // K_PASS
+ROW_TILES = BATCH // P
+N_TILE = 512
+CHUNK = 1024
+N_TILES = CHUNK // N_TILE
+PAIRS = HID // CHUNK
+CHUNKS = GATES // CHUNK
+M_SCALE = 1.5
+
+FLOPS = 2 * BATCH * K_ALL * GATES
+
+
+def tile_koslmcell_pa_kernel(
+    tc, x, h_prev, c_prev, W_ih_words, W_ih_scales, b_ih, W_hh_words, W_hh_scales, b_hh,
+    log_lambda, z_bias, m_bias, out_0, out_1, out_2,
+):
+    nc = tc.nc
+    with ExitStack() as ctx:
+        keep = ctx.enter_context(tc.tile_pool(name="keep", bufs=1))
+        psum = ctx.enter_context(tc.psum_pool(name="psum", bufs=8))
+
+        act_sb = keep.tile([P, ROW_TILES, K_ALL], BF16)
+        c_sb = keep.tile([P, ROW_TILES, HID], BF16)
+        grouped = keep.tile([P, PASSES, ROW_TILES, K_PASS], BF16, align_bytes=64)
+        a_codes = keep.tile([P, PASSES, ROW_TILES, P], U32, align_bytes=64)
+        a_scales = keep.tile([P, PASSES, ROW_TILES, P], U8, align_bytes=64)
+        w_words = [keep.tile([P, PASSES, 2 * CHUNK], U8, align_bytes=64, name="w_words%d" % c) for c in range(CHUNKS)]
+        w_scales = [keep.tile([P, PASSES, CHUNK], U8, align_bytes=64, name="w_scales%d" % c) for c in range(CHUNKS)]
+        vec_rows = keep.tile([P, GATES + HID], BF16)
+        ones = keep.tile([P, P], BF16)
+        ident = keep.tile([P, P], F32)
+        bias_all = keep.tile([P, GATES], F32)
+        decay = keep.tile([P, HID], F32)
+        z_sb = keep.tile([P, ROW_TILES, HID], F32)
+        m_sb = keep.tile([P, ROW_TILES, HID], F32)
+        innov_sb = keep.tile([P, ROW_TILES, HID], F32)
+
+        words_of_pass = [(W_ih_words, g) for g in range(X_PASSES)] + [
+            (W_hh_words, g) for g in range(PASSES - X_PASSES)
+        ]
+        chunk_cols = []
+        for pair in range(PAIRS):
+            chunk_cols.append(HID + pair * CHUNK)
+            chunk_cols.append(pair * CHUNK)
+
+        nc.vector.memset(vec_rows[:].bitcast(I32), 0)
+        nc.vector.memset(ones[:], 1.0)
+        for c in range(CHUNKS):
+            nc.vector.memset(w_scales[c][:].rearrange("p g n -> p (g n)").bitcast(I32), 0)
+        make_identity(nc, ident[:])
+
+        def load_chunk(c):
+            col0 = chunk_cols[c]
+            for scales, g0, g1 in ((W_ih_scales, 0, X_PASSES), (W_hh_scales, X_PASSES, PASSES)):
+                by_lane = scales.bitcast(I32).rearrange("g (quad lane) w -> lane quad g w", lane=4)
+                for lane in range(4):
+                    nc.sync.dma_start(
+                        out=w_scales[c][lane:P:32, g0:g1, :].bitcast(I32),
+                        in_=by_lane[lane, :, :, col0 // 4 : (col0 + CHUNK) // 4],
+                    )
+            for g in range(PASSES):
+                words, g_local = words_of_pass[g]
+                nc.sync.dma_start(
+                    out=w_words[c][:, g, :].bitcast(I32),
+                    in_=words.bitcast(I32)[g_local, :, col0 // 2 : (col0 + CHUNK) // 2],
+                )
+
+        with tc.manual_schedule():
+            for r in range(ROW_TILES):
+                nc.sync.dma_start(out=act_sb[:, r, 0:D_IN], in_=x[r * P : (r + 1) * P, :])
+            for r in range(ROW_TILES):
+                nc.sync.dma_start(out=act_sb[:, r, D_IN:K_ALL], in_=h_prev[r * P : (r + 1) * P, :])
+            nc.sync.dma_start(out=vec_rows[0:1, GATES : GATES + HID], in_=log_lambda.unsqueeze(0))
+            nc.sync.dma_start(out=vec_rows[0:1, 0:GATES], in_=b_ih.unsqueeze(0))
+            nc.sync.dma_start(out=vec_rows[1:2, 0:GATES], in_=b_hh.unsqueeze(0))
+            nc.sync.dma_start(out=vec_rows[2:3, 0:HID], in_=z_bias.unsqueeze(0))
+            nc.sync.dma_start(out=vec_rows[2:3, HID:GATES], in_=m_bias.unsqueeze(0))
+            load_chunk(0)
+            for r in range(ROW_TILES):
+                nc.sync.dma_start(out=c_sb[:, r, :], in_=c_prev[r * P : (r + 1) * P, :])
+            for c in range(1, CHUNKS):
+                load_chunk(c)
+
+        for g0 in range(0, PASSES, 2):
+            for r in range(ROW_TILES):
+                act_words = act_sb[:, r, :].bitcast(F32)
+                flipped = psum.tile([P, 2, 2, P], F32, tag="bank")
+                for gg in range(2):
+                    for u in range(2):
+                        w0 = (g0 + gg) * (K_PASS // 2)
+                        nc.tensor.transpose(
+                            flipped[:, gg, u, :], act_words[:, w0 + u : w0 + K_PASS // 2 : 2], ident[:]
+                        )
+                side_by_side = grouped[:, g0 : g0 + 2, r, :].bitcast(F32).rearrange(
+                    "p g (b u) -> p g b u", u=2
+                )
+                if r == 0:
+                    nc.vector.tensor_copy(out=side_by_side, in_=flipped[:].rearrange("p g u b -> p g b u"))
+                else:
+                    nc.scalar.copy(out=side_by_side, in_=flipped[:].rearrange("p g u b -> p g b u"))
+            nc.vector.quantize_mx(
+                out=a_codes[:, g0 : g0 + 2].rearrange("p g r b -> p (g r b)").bitcast(FP8X4),
+                scales=a_scales[:, g0 : g0 + 2].rearrange("p g r b -> p (g r b)"),
+                in_=grouped[:, g0 : g0 + 2].rearrange("p g r k -> p (g r k)"),
+            )
+
+        for n0 in range(0, HID, N_TILE):
+            spread = psum.tile([P, N_TILE], F32, tag="bank")
+            nc.tensor.matmul(
+                spread[:], lhsT=ones[:], rhs=vec_rows[:, GATES + n0 : GATES + n0 + N_TILE], start=True, stop=True
+            )
+            nc.scalar.activation(out=decay[:, n0 : n0 + N_TILE], in_=spread[:], func=ACT.Exp)
+        for c in range(CHUNKS):
+            for nt in range(N_TILES):
+                n0 = chunk_cols[c] + nt * N_TILE
+                spread = psum.tile([P, N_TILE], F32, tag="bank")
+                nc.tensor.matmul(spread[:], lhsT=ones[:], rhs=vec_rows[:, n0 : n0 + N_TILE], start=True, stop=True)
+                nc.scalar.copy(out=bias_all[:, n0 : n0 + N_TILE], in_=spread[:])
+
+        for c in range(CHUNKS):
+            is_m = chunk_cols[c] >= HID
+            for r in range(ROW_TILES):
+                rows = slice(r * P, (r + 1) * P)
+                for nt in range(N_TILES):
+                    gate0 = chunk_cols[c] + nt * N_TILE
+                    gate_cols = slice(gate0, gate0 + N_TILE)
+                    cols = slice(gate0 % HID, gate0 % HID + N_TILE)
+                    acc = psum.tile([P, N_TILE], F32, tag="bank")
+                    for g in range(PASSES):
+                        nc.tensor.matmul_mx(
+                            out=acc[:],
+                            lhsT=a_codes[:, g, r, :].bitcast(FP8X4),
+                            lhsT_scale=a_scales[:, g, r, :],
+                            rhs=w_words[c][:, g, 2 * nt * N_TILE : 2 * (nt + 1) * N_TILE].bitcast(FP4X4),
+                            rhs_scale=w_scales[c][:, g, nt * N_TILE : (nt + 1) * N_TILE],
+                            start=(g == 0),
+                            stop=(g == PASSES - 1),
+                        )
+                    if is_m:
+                        nc.gpsimd.tensor_mul(innov_sb[:, r, cols], c_sb[:, r, cols], decay[:, cols])
+                        nc.vector.tensor_add(out=m_sb[:, r, cols], in0=acc[:], in1=bias_all[:, gate_cols])
+                        nc.scalar.activation(out=m_sb[:, r, cols], in_=m_sb[:, r, cols], func=ACT.Tanh)
+                        nc.scalar.mul(m_sb[:, r, cols], m_sb[:, r, cols], M_SCALE)
+                        nc.sync.dma_start(out=out_1[rows, cols], in_=m_sb[:, r, cols])
+                        nc.vector.tensor_mul(innov_sb[:, r, cols], innov_sb[:, r, cols], m_sb[:, r, cols])
+                    else:
+                        nc.vector.tensor_add(out=z_sb[:, r, cols], in0=acc[:], in1=bias_all[:, gate_cols])
+                        nc.scalar.activation(out=z_sb[:, r, cols], in_=z_sb[:, r, cols], func=ACT.Tanh)
+                        nc.sync.dma_start(out=out_0[rows, cols], in_=z_sb[:, r, cols])
+                        nc.vector.tensor_add(
+                            out=innov_sb[:, r, cols], in0=innov_sb[:, r, cols], in1=z_sb[:, r, cols]
+                        )
+                        nc.sync.dma_start(out=out_2[rows, cols], in_=innov_sb[:, r, cols])

@@ -23,8 +23,8 @@ ROW_TILES = BATCH // P
 N_TILE = 512
 CHUNK = 1024
 N_TILES = CHUNK // N_TILE
-PAIRS = HID // CHUNK
 CHUNKS = GATES // CHUNK
+HALF_CHUNKS = HID // CHUNK
 M_SCALE = 1.5
 
 FLOPS = 2 * BATCH * K_ALL * GATES
@@ -45,7 +45,7 @@ def tile_koslmcell_pa_kernel(
         a_codes = keep.tile([P, PASSES, ROW_TILES, P], U32, align_bytes=64)
         a_scales = keep.tile([P, PASSES, ROW_TILES, P], U8, align_bytes=64)
         w_words = [keep.tile([P, PASSES, 2 * CHUNK], U8, align_bytes=64, name="w_words%d" % c) for c in range(CHUNKS)]
-        w_scales = [keep.tile([P, PASSES, CHUNK], U8, align_bytes=64, name="w_scales%d" % c) for c in range(CHUNKS)]
+        w_scales = [keep.tile([P, PASSES, HID], U8, align_bytes=64, name="w_scales%d" % s) for s in range(2)]
         vec_rows = keep.tile([P, GATES + HID], BF16)
         ones = keep.tile([P, P], BF16)
         ident = keep.tile([P, P], F32)
@@ -58,26 +58,28 @@ def tile_koslmcell_pa_kernel(
         words_of_pass = [(W_ih_words, g) for g in range(X_PASSES)] + [
             (W_hh_words, g) for g in range(PASSES - X_PASSES)
         ]
-        chunk_cols = []
-        for pair in range(PAIRS):
-            chunk_cols.append(HID + pair * CHUNK)
-            chunk_cols.append(pair * CHUNK)
+        half_cols = [HID, 0]
+        chunk_cols = [half_cols[c // HALF_CHUNKS] + (c % HALF_CHUNKS) * CHUNK for c in range(CHUNKS)]
 
         nc.vector.memset(vec_rows[:].bitcast(I32), 0)
         nc.vector.memset(ones[:], 1.0)
-        for c in range(CHUNKS):
-            nc.vector.memset(w_scales[c][:].rearrange("p g n -> p (g n)").bitcast(I32), 0)
+        for s in range(2):
+            nc.vector.memset(w_scales[s][:].rearrange("p g n -> p (g n)").bitcast(I32), 0)
         make_identity(nc, ident[:])
 
-        def load_chunk(c):
-            col0 = chunk_cols[c]
+        def load_scales(s):
+            col0 = half_cols[s]
             for scales, g0, g1 in ((W_ih_scales, 0, X_PASSES), (W_hh_scales, X_PASSES, PASSES)):
-                by_lane = scales.bitcast(I32).rearrange("g (quad lane) w -> lane quad g w", lane=4)
-                for lane in range(4):
+                by_row = scales.bitcast(I32).rearrange("g (two q) w -> q two g w", two=2)
+                for q in range(8):
+                    first = 32 * (q // 4) + q % 4
                     nc.sync.dma_start(
-                        out=w_scales[c][lane:P:32, g0:g1, :].bitcast(I32),
-                        in_=by_lane[lane, :, :, col0 // 4 : (col0 + CHUNK) // 4],
+                        out=w_scales[s][first:P:64, g0:g1, :].bitcast(I32),
+                        in_=by_row[q, :, :, col0 // 4 : (col0 + HID) // 4],
                     )
+
+        def load_words(c):
+            col0 = chunk_cols[c]
             for g in range(PASSES):
                 words, g_local = words_of_pass[g]
                 nc.sync.dma_start(
@@ -95,11 +97,14 @@ def tile_koslmcell_pa_kernel(
             nc.sync.dma_start(out=vec_rows[1:2, 0:GATES], in_=b_hh.unsqueeze(0))
             nc.sync.dma_start(out=vec_rows[2:3, 0:HID], in_=z_bias.unsqueeze(0))
             nc.sync.dma_start(out=vec_rows[2:3, HID:GATES], in_=m_bias.unsqueeze(0))
-            load_chunk(0)
+            load_scales(0)
+            load_words(0)
             for r in range(ROW_TILES):
                 nc.sync.dma_start(out=c_sb[:, r, :], in_=c_prev[r * P : (r + 1) * P, :])
-            for c in range(1, CHUNKS):
-                load_chunk(c)
+            load_words(1)
+            load_scales(1)
+            load_words(2)
+            load_words(3)
 
         for g0 in range(0, PASSES, 2):
             for r in range(ROW_TILES):
@@ -152,7 +157,7 @@ def tile_koslmcell_pa_kernel(
                             lhsT=a_codes[:, g, r, :].bitcast(FP8X4),
                             lhsT_scale=a_scales[:, g, r, :],
                             rhs=w_words[c][:, g, 2 * nt * N_TILE : 2 * (nt + 1) * N_TILE].bitcast(FP4X4),
-                            rhs_scale=w_scales[c][:, g, nt * N_TILE : (nt + 1) * N_TILE],
+                            rhs_scale=w_scales[c // HALF_CHUNKS][:, g, cols],
                             start=(g == 0),
                             stop=(g == PASSES - 1),
                         )

@@ -18,13 +18,11 @@ BATCH, D_IN, HID = 256, 1024, 2048
 GATES = 2 * HID
 K_ALL = D_IN + HID
 PASSES = K_ALL // K_PASS
-X_PASSES = D_IN // K_PASS
+PAIRS = PASSES // 2
 ROW_TILES = BATCH // P
 N_TILE = 512
 CHUNK = 1024
 N_TILES = CHUNK // N_TILE
-CHUNKS = GATES // CHUNK
-HALF_CHUNKS = HID // CHUNK
 M_SCALE = 1.5
 
 FLOPS = 2 * BATCH * K_ALL * GATES
@@ -38,141 +36,205 @@ def tile_koslmcell_pa_kernel(
     with ExitStack() as ctx:
         keep = ctx.enter_context(tc.tile_pool(name="keep", bufs=1))
         psum = ctx.enter_context(tc.psum_pool(name="psum", bufs=8))
+        ctx.enter_context(tc.manual_schedule())
 
-        act_sb = keep.tile([P, ROW_TILES, K_ALL], BF16)
+        chunk_gate0 = [HID, HID + CHUNK, 0, CHUNK]
+        chunks = len(chunk_gate0)
+
+        x_sb = [keep.tile([P, D_IN], BF16, name="x_sb%d" % r) for r in range(ROW_TILES)]
+        h_sb = [keep.tile([P, HID], BF16, name="h_sb%d" % r) for r in range(ROW_TILES)]
         c_sb = keep.tile([P, ROW_TILES, HID], BF16)
-        grouped = keep.tile([P, PASSES, ROW_TILES, K_PASS], BF16, align_bytes=64)
-        a_codes = keep.tile([P, PASSES, ROW_TILES, P], U32, align_bytes=64)
-        a_scales = keep.tile([P, PASSES, ROW_TILES, P], U8, align_bytes=64)
-        w_words = [keep.tile([P, PASSES, 2 * CHUNK], U8, align_bytes=64, name="w_words%d" % c) for c in range(CHUNKS)]
-        w_scales = [keep.tile([P, PASSES, HID], U8, align_bytes=64, name="w_scales%d" % s) for s in range(2)]
-        vec_rows = keep.tile([P, GATES + HID], BF16)
+        grouped = [
+            keep.tile([P, ROW_TILES, 2, K_PASS], BF16, align_bytes=64, name="grouped%d" % i) for i in range(PAIRS)
+        ]
+        a_codes = [keep.tile([P, ROW_TILES, 2, P], U32, align_bytes=64, name="a_codes%d" % i) for i in range(PAIRS)]
+        a_scales = [keep.tile([P, ROW_TILES, 2, P], U8, align_bytes=64, name="a_scales%d" % i) for i in range(PAIRS)]
+        w_words = [
+            [keep.tile([P, 2, 2 * CHUNK], U8, align_bytes=64, name="w_words%d_%d" % (c, i)) for i in range(PAIRS)]
+            for c in range(chunks)
+        ]
+        w_scales = [keep.tile([P, PASSES, CHUNK], U8, align_bytes=64, name="w_scales%d" % c) for c in range(chunks)]
+        vec_m = keep.tile([P, HID], BF16)
+        vec_l = keep.tile([P, HID], BF16)
+        vec_z = keep.tile([P, HID], BF16)
         ones = keep.tile([P, P], BF16)
         ident = keep.tile([P, P], F32)
-        bias_all = keep.tile([P, GATES], F32)
+        warm = keep.tile([P, 1], F32)
+        bias_m = keep.tile([P, HID], F32)
+        bias_z = keep.tile([P, HID], F32)
         decay = keep.tile([P, HID], F32)
         z_sb = keep.tile([P, ROW_TILES, HID], F32)
         m_sb = keep.tile([P, ROW_TILES, HID], F32)
         innov_sb = keep.tile([P, ROW_TILES, HID], F32)
 
-        words_of_pass = [(W_ih_words, g) for g in range(X_PASSES)] + [
-            (W_hh_words, g) for g in range(PASSES - X_PASSES)
-        ]
-        half_cols = [HID, 0]
-        chunk_cols = [half_cols[c // HALF_CHUNKS] + (c % HALF_CHUNKS) * CHUNK for c in range(CHUNKS)]
-
-        nc.vector.memset(vec_rows[:].bitcast(I32), 0)
-        nc.vector.memset(ones[:], 1.0)
-        for s in range(2):
-            nc.vector.memset(w_scales[s][:].rearrange("p g n -> p (g n)").bitcast(I32), 0)
+        nc.gpsimd.memset(warm[:], 0.0)
+        nc.scalar.activation(out=warm[:], in_=warm[:], func=ACT.Exp)
+        nc.vector.memset(vec_m[:].bitcast(I32), 0)
+        nc.vector.memset(w_scales[0][:].rearrange("p g n -> p (g n)").bitcast(I32), 0)
+        nc.gpsimd.memset(ones[:], 1.0)
         make_identity(nc, ident[:])
+        nc.vector.memset(vec_l[:].bitcast(I32), 0)
+        nc.vector.memset(w_scales[1][:].rearrange("p g n -> p (g n)").bitcast(I32), 0)
+        nc.vector.memset(vec_z[:].bitcast(I32), 0)
+        nc.vector.memset(w_scales[2][:].rearrange("p g n -> p (g n)").bitcast(I32), 0)
+        nc.vector.memset(w_scales[3][:].rearrange("p g n -> p (g n)").bitcast(I32), 0)
 
-        def load_scales(s):
-            col0 = half_cols[s]
-            for scales, g0, g1 in ((W_ih_scales, 0, X_PASSES), (W_hh_scales, X_PASSES, PASSES)):
-                by_row = scales.bitcast(I32).rearrange("g (two q) w -> q two g w", two=2)
-                for q in range(8):
-                    first = 32 * (q // 4) + q % 4
+        def load_scales(c):
+            col0 = chunk_gate0[c]
+            for scales, g0, g1 in ((W_ih_scales, 0, 2), (W_hh_scales, 2, PASSES)):
+                by_row = scales.bitcast(I32).rearrange("g (q j) w -> j q g w", j=4)
+                for j in range(4):
                     nc.sync.dma_start(
-                        out=w_scales[s][first:P:64, g0:g1, :].bitcast(I32),
-                        in_=by_row[q, :, :, col0 // 4 : (col0 + HID) // 4],
+                        out=w_scales[c][j:P:32, g0:g1, :].bitcast(I32),
+                        in_=by_row[j, :, :, col0 // 4 : (col0 + CHUNK) // 4],
                     )
 
         def load_words(c):
-            col0 = chunk_cols[c]
-            for g in range(PASSES):
-                words, g_local = words_of_pass[g]
+            col0 = chunk_gate0[c]
+            for i in range(PAIRS):
+                words = W_ih_words if i == 0 else W_hh_words
+                g0 = 0 if i == 0 else 2 * (i - 1)
                 nc.sync.dma_start(
-                    out=w_words[c][:, g, :].bitcast(I32),
-                    in_=words.bitcast(I32)[g_local, :, col0 // 2 : (col0 + CHUNK) // 2],
+                    out=w_words[c][i][:].bitcast(I32),
+                    in_=words.bitcast(I32).rearrange("g p w -> p g w")[
+                        :, g0 : g0 + 2, col0 // 2 : (col0 + CHUNK) // 2
+                    ],
                 )
 
-        with tc.manual_schedule():
-            for r in range(ROW_TILES):
-                nc.sync.dma_start(out=act_sb[:, r, 0:D_IN], in_=x[r * P : (r + 1) * P, :])
-            for r in range(ROW_TILES):
-                nc.sync.dma_start(out=act_sb[:, r, D_IN:K_ALL], in_=h_prev[r * P : (r + 1) * P, :])
-            nc.sync.dma_start(out=vec_rows[0:1, GATES : GATES + HID], in_=log_lambda.unsqueeze(0))
-            nc.sync.dma_start(out=vec_rows[0:1, 0:GATES], in_=b_ih.unsqueeze(0))
-            nc.sync.dma_start(out=vec_rows[1:2, 0:GATES], in_=b_hh.unsqueeze(0))
-            nc.sync.dma_start(out=vec_rows[2:3, 0:HID], in_=z_bias.unsqueeze(0))
-            nc.sync.dma_start(out=vec_rows[2:3, HID:GATES], in_=m_bias.unsqueeze(0))
-            load_scales(0)
-            load_words(0)
-            for r in range(ROW_TILES):
-                nc.sync.dma_start(out=c_sb[:, r, :], in_=c_prev[r * P : (r + 1) * P, :])
-            load_words(1)
-            load_scales(1)
-            load_words(2)
-            load_words(3)
+        for r in range(ROW_TILES):
+            nc.sync.dma_start(out=x_sb[r][:], in_=x[r * P : (r + 1) * P, :])
+        for r in range(ROW_TILES):
+            nc.sync.dma_start(out=h_sb[r][:], in_=h_prev[r * P : (r + 1) * P, :])
+        nc.scalar.dma_start(out=vec_m[4:5, :], in_=b_ih[HID:GATES].unsqueeze(0))
+        nc.scalar.dma_start(out=vec_m[8:9, :], in_=b_hh[HID:GATES].unsqueeze(0))
+        nc.scalar.dma_start(out=vec_m[12:13, :], in_=m_bias.unsqueeze(0))
+        nc.scalar.dma_start(out=vec_l[4:5, :], in_=log_lambda.unsqueeze(0))
+        nc.scalar.dma_start(out=vec_z[4:5, :], in_=b_ih[0:HID].unsqueeze(0))
+        nc.scalar.dma_start(out=vec_z[8:9, :], in_=b_hh[0:HID].unsqueeze(0))
+        nc.scalar.dma_start(out=vec_z[12:13, :], in_=z_bias.unsqueeze(0))
+        load_scales(0)
+        load_words(0)
+        load_scales(1)
+        load_words(1)
+        for r in range(ROW_TILES):
+            nc.sync.dma_start(out=c_sb[:, r, :], in_=c_prev[r * P : (r + 1) * P, :])
+        load_scales(2)
+        load_words(2)
+        load_scales(3)
+        load_words(3)
 
-        for g0 in range(0, PASSES, 2):
-            for r in range(ROW_TILES):
-                act_words = act_sb[:, r, :].bitcast(F32)
-                flipped = psum.tile([P, 2, 2, P], F32, tag="bank")
-                for gg in range(2):
-                    for u in range(2):
-                        w0 = (g0 + gg) * (K_PASS // 2)
-                        nc.tensor.transpose(
-                            flipped[:, gg, u, :], act_words[:, w0 + u : w0 + K_PASS // 2 : 2], ident[:]
-                        )
-                side_by_side = grouped[:, g0 : g0 + 2, r, :].bitcast(F32).rearrange(
-                    "p g (b u) -> p g b u", u=2
-                )
-                if r == 0:
-                    nc.vector.tensor_copy(out=side_by_side, in_=flipped[:].rearrange("p g u b -> p g b u"))
-                else:
-                    nc.scalar.copy(out=side_by_side, in_=flipped[:].rearrange("p g u b -> p g b u"))
+        def flip(i, r):
+            src = x_sb[r] if i == 0 else h_sb[r]
+            base = 0 if i == 0 else (i - 1) * K_PASS
+            src_words = src[:].bitcast(F32)
+            flipped = psum.tile([P, 2, 2, P], F32, tag="bank")
+            for gg in range(2):
+                for u in range(2):
+                    w0 = base + gg * (K_PASS // 2)
+                    nc.tensor.transpose(flipped[:, gg, u, :], src_words[:, w0 + u : w0 + K_PASS // 2 : 2], ident[:])
+            side_by_side = grouped[i][:, r, :, :].bitcast(F32).rearrange("p g (b u) -> p g b u", u=2)
+            if r == 0:
+                nc.vector.tensor_copy(out=side_by_side, in_=flipped[:].rearrange("p g u b -> p g b u"))
+            else:
+                nc.scalar.copy(out=side_by_side, in_=flipped[:].rearrange("p g u b -> p g b u"))
+
+        def quantise(i):
             nc.vector.quantize_mx(
-                out=a_codes[:, g0 : g0 + 2].rearrange("p g r b -> p (g r b)").bitcast(FP8X4),
-                scales=a_scales[:, g0 : g0 + 2].rearrange("p g r b -> p (g r b)"),
-                in_=grouped[:, g0 : g0 + 2].rearrange("p g r k -> p (g r k)"),
+                out=a_codes[i][:].rearrange("p r g b -> p (r g b)").bitcast(FP8X4),
+                scales=a_scales[i][:].rearrange("p r g b -> p (r g b)"),
+                in_=grouped[i][:].rearrange("p r g k -> p (r g k)"),
             )
 
+        def spread(vec, n0):
+            bank = psum.tile([P, N_TILE], F32, tag="bank")
+            nc.tensor.matmul(bank[:], lhsT=ones[:], rhs=vec[:, n0 : n0 + N_TILE], start=True, stop=True)
+            return bank
+
+        flip(0, 0)
+        flip(0, 1)
+        quantise(0)
         for n0 in range(0, HID, N_TILE):
-            spread = psum.tile([P, N_TILE], F32, tag="bank")
-            nc.tensor.matmul(
-                spread[:], lhsT=ones[:], rhs=vec_rows[:, GATES + n0 : GATES + n0 + N_TILE], start=True, stop=True
-            )
-            nc.scalar.activation(out=decay[:, n0 : n0 + N_TILE], in_=spread[:], func=ACT.Exp)
-        for c in range(CHUNKS):
-            for nt in range(N_TILES):
-                n0 = chunk_cols[c] + nt * N_TILE
-                spread = psum.tile([P, N_TILE], F32, tag="bank")
-                nc.tensor.matmul(spread[:], lhsT=ones[:], rhs=vec_rows[:, n0 : n0 + N_TILE], start=True, stop=True)
-                nc.scalar.copy(out=bias_all[:, n0 : n0 + N_TILE], in_=spread[:])
+            bank = spread(vec_m, n0)
+            nc.scalar.copy(out=bias_m[:, n0 : n0 + N_TILE], in_=bank[:])
+        flip(1, 0)
+        flip(1, 1)
+        flip(2, 0)
+        flip(2, 1)
+        quantise(1)
+        quantise(2)
+        for n0 in range(0, HID, N_TILE):
+            bank = spread(vec_l, n0)
+            nc.scalar.activation(out=decay[:, n0 : n0 + N_TILE], in_=bank[:], func=ACT.Exp)
 
-        for c in range(CHUNKS):
-            is_m = chunk_cols[c] >= HID
-            for r in range(ROW_TILES):
+        def mx_pass(acc, c, r, nt, g):
+            nc.tensor.matmul_mx(
+                out=acc[:],
+                lhsT=a_codes[g // 2][:, r, g % 2, :].bitcast(FP8X4),
+                lhsT_scale=a_scales[g // 2][:, r, g % 2, :],
+                rhs=w_words[c][g // 2][:, g % 2, 2 * nt * N_TILE : 2 * (nt + 1) * N_TILE].bitcast(FP4X4),
+                rhs_scale=w_scales[c][:, g, nt * N_TILE : (nt + 1) * N_TILE],
+                start=(g == 0),
+                stop=(g == PASSES - 1),
+            )
+
+        banks_of_chunk = [(r, nt) for r in range(ROW_TILES) for nt in range(N_TILES)]
+
+        def out_cols(c, nt):
+            col0 = chunk_gate0[c] % HID + nt * N_TILE
+            return slice(col0, col0 + N_TILE)
+
+        def c_times_decay(c, r, nt):
+            cols = out_cols(c, nt)
+            nc.gpsimd.tensor_mul(innov_sb[:, r, cols], c_sb[:, r, cols], decay[:, cols])
+
+        def times_m(c, r, nt):
+            cols = out_cols(c, nt)
+            nc.vector.tensor_mul(innov_sb[:, r, cols], innov_sb[:, r, cols], m_sb[:, r, cols])
+
+        for c in range(2):
+            accs = []
+            for b in range(len(banks_of_chunk)):
+                acc = psum.tile([P, N_TILE], F32, tag="bank")
+                accs.append(acc)
+            for g in range(2):
+                for b, (r, nt) in enumerate(banks_of_chunk):
+                    mx_pass(accs[b], c, r, nt, g)
+            for b, (r, nt) in enumerate(banks_of_chunk):
+                cols = out_cols(c, nt)
+                for g in range(2, PASSES):
+                    mx_pass(accs[b], c, r, nt, g)
+                nc.vector.tensor_add(out=m_sb[:, r, cols], in0=accs[b][:], in1=bias_m[:, cols])
+                nc.scalar.activation(out=m_sb[:, r, cols], in_=m_sb[:, r, cols], func=ACT.Tanh)
+                nc.scalar.mul(m_sb[:, r, cols], m_sb[:, r, cols], M_SCALE)
+                if c == 1:
+                    times_m(0, r, nt)
+                if nt == N_TILES - 1:
+                    wide = slice(chunk_gate0[c] % HID, chunk_gate0[c] % HID + CHUNK)
+                    nc.sync.dma_start(out=out_1[r * P : (r + 1) * P, wide], in_=m_sb[:, r, wide])
+            if c == 0:
+                z_banks = [spread(vec_z, n0) for n0 in range(0, HID, N_TILE)]
+                for n, bank in enumerate(z_banks):
+                    nc.scalar.copy(out=bias_z[:, n * N_TILE : (n + 1) * N_TILE], in_=bank[:])
+            for r, nt in banks_of_chunk:
+                c_times_decay(c, r, nt)
+
+        for c in range(2, chunks):
+            for r, nt in banks_of_chunk:
+                cols = out_cols(c, nt)
                 rows = slice(r * P, (r + 1) * P)
-                for nt in range(N_TILES):
-                    gate0 = chunk_cols[c] + nt * N_TILE
-                    gate_cols = slice(gate0, gate0 + N_TILE)
-                    cols = slice(gate0 % HID, gate0 % HID + N_TILE)
-                    acc = psum.tile([P, N_TILE], F32, tag="bank")
-                    for g in range(PASSES):
-                        nc.tensor.matmul_mx(
-                            out=acc[:],
-                            lhsT=a_codes[:, g, r, :].bitcast(FP8X4),
-                            lhsT_scale=a_scales[:, g, r, :],
-                            rhs=w_words[c][:, g, 2 * nt * N_TILE : 2 * (nt + 1) * N_TILE].bitcast(FP4X4),
-                            rhs_scale=w_scales[c // HALF_CHUNKS][:, g, cols],
-                            start=(g == 0),
-                            stop=(g == PASSES - 1),
-                        )
-                    if is_m:
-                        nc.gpsimd.tensor_mul(innov_sb[:, r, cols], c_sb[:, r, cols], decay[:, cols])
-                        nc.vector.tensor_add(out=m_sb[:, r, cols], in0=acc[:], in1=bias_all[:, gate_cols])
-                        nc.scalar.activation(out=m_sb[:, r, cols], in_=m_sb[:, r, cols], func=ACT.Tanh)
-                        nc.scalar.mul(m_sb[:, r, cols], m_sb[:, r, cols], M_SCALE)
-                        nc.sync.dma_start(out=out_1[rows, cols], in_=m_sb[:, r, cols])
-                        nc.vector.tensor_mul(innov_sb[:, r, cols], innov_sb[:, r, cols], m_sb[:, r, cols])
-                    else:
-                        nc.vector.tensor_add(out=z_sb[:, r, cols], in0=acc[:], in1=bias_all[:, gate_cols])
-                        nc.scalar.activation(out=z_sb[:, r, cols], in_=z_sb[:, r, cols], func=ACT.Tanh)
-                        nc.sync.dma_start(out=out_0[rows, cols], in_=z_sb[:, r, cols])
-                        nc.vector.tensor_add(
-                            out=innov_sb[:, r, cols], in0=innov_sb[:, r, cols], in1=z_sb[:, r, cols]
-                        )
-                        nc.sync.dma_start(out=out_2[rows, cols], in_=innov_sb[:, r, cols])
+                acc = psum.tile([P, N_TILE], F32, tag="bank")
+                for g in range(PASSES):
+                    mx_pass(acc, c, r, nt, g)
+                nc.vector.tensor_add(out=z_sb[:, r, cols], in0=acc[:], in1=bias_z[:, cols])
+                if c == 2:
+                    times_m(1, r, nt)
+                nc.scalar.activation(out=z_sb[:, r, cols], in_=z_sb[:, r, cols], func=ACT.Tanh)
+                nc.vector.tensor_add(out=innov_sb[:, r, cols], in0=innov_sb[:, r, cols], in1=z_sb[:, r, cols])
+                last_rows = c == chunks - 1 and r == ROW_TILES - 1
+                if last_rows:
+                    nc.sync.dma_start(out=out_0[rows, cols], in_=z_sb[:, r, cols])
+                    nc.sync.dma_start(out=out_2[rows, cols], in_=innov_sb[:, r, cols])
+                elif nt == N_TILES - 1:
+                    wide = slice(chunk_gate0[c] % HID, chunk_gate0[c] % HID + CHUNK)
+                    nc.sync.dma_start(out=out_0[rows, wide], in_=z_sb[:, r, wide])
+                    nc.sync.dma_start(out=out_2[rows, wide], in_=innov_sb[:, r, wide])

@@ -178,18 +178,41 @@ def tile_koslmcell_pa_kernel(
             )
 
         banks_of_chunk = [(r, nt) for r in range(ROW_TILES) for nt in range(N_TILES)]
+        banks = [(c, r, nt) for c in range(chunks) for r, nt in banks_of_chunk]
+        m_banks = len(banks) // 2
 
         def out_cols(c, nt):
             col0 = chunk_gate0[c] % HID + nt * N_TILE
             return slice(col0, col0 + N_TILE)
 
-        def c_times_decay(c, r, nt):
+        def finish(i, acc):
+            c, r, nt = banks[i]
             cols = out_cols(c, nt)
-            nc.gpsimd.tensor_mul(innov_sb[:, r, cols], c_sb[:, r, cols], decay[:, cols])
-
-        def times_m(c, r, nt):
-            cols = out_cols(c, nt)
-            nc.vector.tensor_mul(innov_sb[:, r, cols], innov_sb[:, r, cols], m_sb[:, r, cols])
+            rows = slice(r * P, (r + 1) * P)
+            wide = slice(chunk_gate0[c] % HID, chunk_gate0[c] % HID + CHUNK)
+            is_m = i < m_banks
+            last = i == len(banks) - 1
+            res = m_sb if is_m else z_sb
+            nc.vector.tensor_add(out=res[:, r, cols], in0=acc[:], in1=(bias_m if is_m else bias_z)[:, cols])
+            if 4 <= i < 4 + m_banks:
+                c4, r4, nt4 = banks[i - 4]
+                cols4 = out_cols(c4, nt4)
+                nc.vector.tensor_mul(innov_sb[:, r4, cols4], innov_sb[:, r4, cols4], c_sb[:, r4, cols4])
+            nc.scalar.activation(out=res[:, r, cols], in_=res[:, r, cols], func=ACT.Tanh)
+            if is_m:
+                nc.scalar.mul(m_sb[:, r, cols], m_sb[:, r, cols], M_SCALE)
+                nc.gpsimd.tensor_mul(innov_sb[:, r, cols], m_sb[:, r, cols], decay[:, cols])
+                if nt == N_TILES - 1:
+                    nc.sync.dma_start(out=out_1[rows, wide], in_=m_sb[:, r, wide])
+                return
+            adder = nc.vector if last else nc.gpsimd
+            adder.tensor_add(out=innov_sb[:, r, cols], in0=innov_sb[:, r, cols], in1=z_sb[:, r, cols])
+            if c == chunks - 1 and r == ROW_TILES - 1:
+                nc.sync.dma_start(out=out_0[rows, cols], in_=z_sb[:, r, cols])
+                nc.sync.dma_start(out=out_2[rows, cols], in_=innov_sb[:, r, cols])
+            elif nt == N_TILES - 1:
+                nc.sync.dma_start(out=out_0[rows, wide], in_=z_sb[:, r, wide])
+                nc.sync.dma_start(out=out_2[rows, wide], in_=innov_sb[:, r, wide])
 
         for c in range(2):
             accs = []
@@ -200,41 +223,17 @@ def tile_koslmcell_pa_kernel(
                 for b, (r, nt) in enumerate(banks_of_chunk):
                     mx_pass(accs[b], c, r, nt, g)
             for b, (r, nt) in enumerate(banks_of_chunk):
-                cols = out_cols(c, nt)
                 for g in range(2, PASSES):
                     mx_pass(accs[b], c, r, nt, g)
-                nc.vector.tensor_add(out=m_sb[:, r, cols], in0=accs[b][:], in1=bias_m[:, cols])
-                nc.scalar.activation(out=m_sb[:, r, cols], in_=m_sb[:, r, cols], func=ACT.Tanh)
-                nc.scalar.mul(m_sb[:, r, cols], m_sb[:, r, cols], M_SCALE)
-                if c == 1:
-                    times_m(0, r, nt)
-                if nt == N_TILES - 1:
-                    wide = slice(chunk_gate0[c] % HID, chunk_gate0[c] % HID + CHUNK)
-                    nc.sync.dma_start(out=out_1[r * P : (r + 1) * P, wide], in_=m_sb[:, r, wide])
+                finish(c * len(banks_of_chunk) + b, accs[b])
             if c == 0:
                 z_banks = [spread(vec_z, n0) for n0 in range(0, HID, N_TILE)]
                 for n, bank in enumerate(z_banks):
                     nc.scalar.copy(out=bias_z[:, n * N_TILE : (n + 1) * N_TILE], in_=bank[:])
-            for r, nt in banks_of_chunk:
-                c_times_decay(c, r, nt)
 
         for c in range(2, chunks):
-            for r, nt in banks_of_chunk:
-                cols = out_cols(c, nt)
-                rows = slice(r * P, (r + 1) * P)
+            for b, (r, nt) in enumerate(banks_of_chunk):
                 acc = psum.tile([P, N_TILE], F32, tag="bank")
                 for g in range(PASSES):
                     mx_pass(acc, c, r, nt, g)
-                nc.vector.tensor_add(out=z_sb[:, r, cols], in0=acc[:], in1=bias_z[:, cols])
-                if c == 2:
-                    times_m(1, r, nt)
-                nc.scalar.activation(out=z_sb[:, r, cols], in_=z_sb[:, r, cols], func=ACT.Tanh)
-                nc.vector.tensor_add(out=innov_sb[:, r, cols], in0=innov_sb[:, r, cols], in1=z_sb[:, r, cols])
-                last_rows = c == chunks - 1 and r == ROW_TILES - 1
-                if last_rows:
-                    nc.sync.dma_start(out=out_0[rows, cols], in_=z_sb[:, r, cols])
-                    nc.sync.dma_start(out=out_2[rows, cols], in_=innov_sb[:, r, cols])
-                elif nt == N_TILES - 1:
-                    wide = slice(chunk_gate0[c] % HID, chunk_gate0[c] % HID + CHUNK)
-                    nc.sync.dma_start(out=out_0[rows, wide], in_=z_sb[:, r, wide])
-                    nc.sync.dma_start(out=out_2[rows, wide], in_=innov_sb[:, r, wide])
+                finish(c * len(banks_of_chunk) + b, acc)

@@ -18,11 +18,13 @@ BATCH, D_IN, HID = 256, 1024, 2048
 GATES = 2 * HID
 K_ALL = D_IN + HID
 PASSES = K_ALL // K_PASS
+X_PASSES = D_IN // K_PASS
 PAIRS = PASSES // 2
 ROW_TILES = BATCH // P
 N_TILE = 512
 CHUNK = 1024
 N_TILES = CHUNK // N_TILE
+NARROW = 128
 M_SCALE = 1.5
 
 FLOPS = 2 * BATCH * K_ALL * GATES
@@ -42,22 +44,25 @@ def tile_koslmcell_pa_kernel(
         chunks = len(chunk_gate0)
 
         x_sb = [keep.tile([P, D_IN], BF16, name="x_sb%d" % r) for r in range(ROW_TILES)]
-        h_sb = [keep.tile([P, HID], BF16, name="h_sb%d" % r) for r in range(ROW_TILES)]
+        h_sb = keep.tile([P, ROW_TILES, HID], BF16)
         c_sb = keep.tile([P, ROW_TILES, HID], BF16)
         grouped = [
             keep.tile([P, ROW_TILES, 2, K_PASS], BF16, align_bytes=64, name="grouped%d" % i) for i in range(PAIRS)
         ]
         a_codes = [keep.tile([P, ROW_TILES, 2, P], U32, align_bytes=64, name="a_codes%d" % i) for i in range(PAIRS)]
         a_scales = [keep.tile([P, ROW_TILES, 2, P], U8, align_bytes=64, name="a_scales%d" % i) for i in range(PAIRS)]
+        w_passes = (X_PASSES, PASSES - X_PASSES)
         w_words = [
-            [keep.tile([P, 2, 2 * CHUNK], U8, align_bytes=64, name="w_words%d_%d" % (c, i)) for i in range(PAIRS)]
+            [keep.tile([P, w_passes[s], 2 * CHUNK], U8, align_bytes=64, name="w_words%d_%d" % (c, s)) for s in range(2)]
             for c in range(chunks)
         ]
-        w_scales = [keep.tile([P, PASSES, CHUNK], U8, align_bytes=64, name="w_scales%d" % c) for c in range(chunks)]
-        vec_m = keep.tile([P, HID], BF16)
-        vec_l = keep.tile([P, HID], BF16)
-        vec_z = keep.tile([P, HID], BF16)
-        ones = keep.tile([P, P], BF16)
+        w_scales = [
+            [keep.tile([P, w_passes[s], CHUNK], U8, align_bytes=64, name="w_scales%d_%d" % (c, s)) for s in range(2)]
+            for c in range(chunks)
+        ]
+        vec_rows = keep.tile([P, N_TILE], BF16)
+        pick = keep.tile([P, 12], BF16)
+        pick_sum = keep.tile([P, 8], F32)
         ident = keep.tile([P, P], F32)
         warm = keep.tile([P, 1], F32)
         bias_m = keep.tile([P, HID], F32)
@@ -67,66 +72,56 @@ def tile_koslmcell_pa_kernel(
         m_sb = keep.tile([P, ROW_TILES, HID], F32)
         innov_sb = keep.tile([P, ROW_TILES, HID], F32)
 
+        nc.vector.memset(vec_rows[:].bitcast(I32), 0)
+        make_identity(nc, ident[:])
         nc.gpsimd.memset(warm[:], 0.0)
         nc.scalar.activation(out=warm[:], in_=warm[:], func=ACT.Exp)
-        nc.vector.memset(vec_m[:].bitcast(I32), 0)
-        nc.vector.memset(w_scales[0][:].rearrange("p g n -> p (g n)").bitcast(I32), 0)
-        nc.gpsimd.memset(ones[:], 1.0)
-        make_identity(nc, ident[:])
-        nc.vector.memset(vec_l[:].bitcast(I32), 0)
-        nc.vector.memset(w_scales[1][:].rearrange("p g n -> p (g n)").bitcast(I32), 0)
-        nc.vector.memset(vec_z[:].bitcast(I32), 0)
-        nc.vector.memset(w_scales[2][:].rearrange("p g n -> p (g n)").bitcast(I32), 0)
-        nc.vector.memset(w_scales[3][:].rearrange("p g n -> p (g n)").bitcast(I32), 0)
+        nc.vector.memset(w_scales[0][0][:].rearrange("p g n -> p (g n)").bitcast(I32), 0)
+        nc.vector.tensor_add(out=pick_sum[:], in0=ident[:, 0:8], in1=ident[:, 8:16])
+        nc.vector.tensor_add(out=pick[:, 0:8], in0=pick_sum[:], in1=ident[:, 16:24])
+        nc.vector.tensor_copy(out=pick[:, 8:12], in_=ident[:, 24:28])
+        nc.vector.memset(w_scales[0][1][:].rearrange("p g n -> p (g n)").bitcast(I32), 0)
 
-        def load_scales(c):
+        def load_scales(c, s):
             col0 = chunk_gate0[c]
-            for scales, g0, g1 in ((W_ih_scales, 0, 2), (W_hh_scales, 2, PASSES)):
-                by_row = scales.bitcast(I32).rearrange("g (q j) w -> j q g w", j=4)
-                for j in range(4):
-                    nc.sync.dma_start(
-                        out=w_scales[c][j:P:32, g0:g1, :].bitcast(I32),
-                        in_=by_row[j, :, :, col0 // 4 : (col0 + CHUNK) // 4],
-                    )
-
-        def load_words(c):
-            col0 = chunk_gate0[c]
-            for i in range(PAIRS):
-                words = W_ih_words if i == 0 else W_hh_words
-                g0 = 0 if i == 0 else 2 * (i - 1)
+            by_row = (W_ih_scales, W_hh_scales)[s].bitcast(I32).rearrange("g (q j) w -> j q g w", j=4)
+            for j in range(4):
                 nc.sync.dma_start(
-                    out=w_words[c][i][:].bitcast(I32),
-                    in_=words.bitcast(I32).rearrange("g p w -> p g w")[
-                        :, g0 : g0 + 2, col0 // 2 : (col0 + CHUNK) // 2
-                    ],
+                    out=w_scales[c][s][j:P:32, :, :].bitcast(I32),
+                    in_=by_row[j, :, :, col0 // 4 : (col0 + CHUNK) // 4],
                 )
+
+        def load_words(c, s):
+            col0 = chunk_gate0[c]
+            nc.sync.dma_start(
+                out=w_words[c][s][:].bitcast(I32),
+                in_=(W_ih_words, W_hh_words)[s].bitcast(I32).rearrange("g p w -> p g w")[
+                    :, :, col0 // 2 : (col0 + CHUNK) // 2
+                ],
+            )
 
         for r in range(ROW_TILES):
             nc.sync.dma_start(out=x_sb[r][:], in_=x[r * P : (r + 1) * P, :])
-        for r in range(ROW_TILES):
-            nc.sync.dma_start(out=h_sb[r][:], in_=h_prev[r * P : (r + 1) * P, :])
-        nc.scalar.dma_start(out=vec_m[4:5, :], in_=b_ih[HID:GATES].unsqueeze(0))
-        nc.scalar.dma_start(out=vec_m[8:9, :], in_=b_hh[HID:GATES].unsqueeze(0))
-        nc.scalar.dma_start(out=vec_m[12:13, :], in_=m_bias.unsqueeze(0))
-        nc.scalar.dma_start(out=vec_l[4:5, :], in_=log_lambda.unsqueeze(0))
-        nc.scalar.dma_start(out=vec_z[4:5, :], in_=b_ih[0:HID].unsqueeze(0))
-        nc.scalar.dma_start(out=vec_z[8:9, :], in_=b_hh[0:HID].unsqueeze(0))
-        nc.scalar.dma_start(out=vec_z[12:13, :], in_=z_bias.unsqueeze(0))
-        load_scales(0)
-        load_words(0)
-        load_scales(1)
-        load_words(1)
-        for r in range(ROW_TILES):
-            nc.sync.dma_start(out=c_sb[:, r, :], in_=c_prev[r * P : (r + 1) * P, :])
-        load_scales(2)
-        load_words(2)
-        load_scales(3)
-        load_words(3)
+        for row0, vec in ((0, b_ih), (8, b_hh), (16, z_bias), (20, m_bias), (24, log_lambda)):
+            by_tile = vec.rearrange("(j n) -> j n", n=N_TILE)
+            nc.sync.dma_start(out=vec_rows[row0 : row0 + by_tile.shape[0], :], in_=by_tile)
+        load_scales(0, 0)
+        load_words(0, 0)
+        nc.sync.dma_start(out=h_sb[:], in_=h_prev.rearrange("(r p) k -> p r k", p=P))
+        load_scales(0, 1)
+        load_words(0, 1)
+
+        def load_chunk(c):
+            for s in range(2):
+                nc.vector.memset(w_scales[c][s][:].rearrange("p g n -> p (g n)").bitcast(I32), 0)
+            for s in range(2):
+                load_scales(c, s)
+            for s in range(2):
+                load_words(c, s)
 
         def flip(i, r):
-            src = x_sb[r] if i == 0 else h_sb[r]
             base = 0 if i == 0 else (i - 1) * K_PASS
-            src_words = src[:].bitcast(F32)
+            src_words = (x_sb[r][:] if i == 0 else h_sb[:, r, :]).bitcast(F32)
             flipped = psum.tile([P, 2, 2, P], F32, tag="bank")
             for gg in range(2):
                 for u in range(2):
@@ -145,34 +140,29 @@ def tile_koslmcell_pa_kernel(
                 in_=grouped[i][:].rearrange("p r g k -> p (r g k)"),
             )
 
-        def spread(vec, n0):
+        def spread(j):
             bank = psum.tile([P, N_TILE], F32, tag="bank")
-            nc.tensor.matmul(bank[:], lhsT=ones[:], rhs=vec[:, n0 : n0 + N_TILE], start=True, stop=True)
+            nc.tensor.matmul(
+                bank[:], lhsT=pick[:, j : j + 1].to_broadcast([P, P]), rhs=vec_rows[:], start=True, stop=True
+            )
             return bank
 
-        flip(0, 0)
-        flip(0, 1)
-        quantise(0)
-        for n0 in range(0, HID, N_TILE):
-            bank = spread(vec_m, n0)
-            nc.scalar.copy(out=bias_m[:, n0 : n0 + N_TILE], in_=bank[:])
-        flip(1, 0)
-        flip(1, 1)
-        flip(2, 0)
-        flip(2, 1)
-        quantise(1)
-        quantise(2)
-        for n0 in range(0, HID, N_TILE):
-            bank = spread(vec_l, n0)
-            nc.scalar.activation(out=decay[:, n0 : n0 + N_TILE], in_=bank[:], func=ACT.Exp)
+        def spread_bias(bias, j0, t):
+            bank = spread(j0 + t)
+            if t % 2 == 0:
+                nc.vector.tensor_copy(out=bias[:, t * N_TILE : (t + 1) * N_TILE], in_=bank[:])
+            else:
+                nc.scalar.copy(out=bias[:, t * N_TILE : (t + 1) * N_TILE], in_=bank[:])
 
         def mx_pass(acc, c, r, nt, g):
+            s = 0 if g < X_PASSES else 1
+            g_local = g - s * X_PASSES
             nc.tensor.matmul_mx(
                 out=acc[:],
                 lhsT=a_codes[g // 2][:, r, g % 2, :].bitcast(FP8X4),
                 lhsT_scale=a_scales[g // 2][:, r, g % 2, :],
-                rhs=w_words[c][g // 2][:, g % 2, 2 * nt * N_TILE : 2 * (nt + 1) * N_TILE].bitcast(FP4X4),
-                rhs_scale=w_scales[c][:, g, nt * N_TILE : (nt + 1) * N_TILE],
+                rhs=w_words[c][s][:, g_local, 2 * nt * N_TILE : 2 * (nt + 1) * N_TILE].bitcast(FP4X4),
+                rhs_scale=w_scales[c][s][:, g_local, nt * N_TILE : (nt + 1) * N_TILE],
                 start=(g == 0),
                 stop=(g == PASSES - 1),
             )
@@ -185,13 +175,22 @@ def tile_koslmcell_pa_kernel(
             col0 = chunk_gate0[c] % HID + nt * N_TILE
             return slice(col0, col0 + N_TILE)
 
+        def last_sum(engine, i, cols):
+            c, r, nt = banks[i]
+            engine.tensor_add(out=innov_sb[:, r, cols], in0=innov_sb[:, r, cols], in1=z_sb[:, r, cols])
+
+        def store_z(i, cols):
+            c, r, nt = banks[i]
+            rows = slice(r * P, (r + 1) * P)
+            nc.sync.dma_start(out=out_0[rows, cols], in_=z_sb[:, r, cols])
+            nc.sync.dma_start(out=out_2[rows, cols], in_=innov_sb[:, r, cols])
+
         def finish(i, acc):
             c, r, nt = banks[i]
             cols = out_cols(c, nt)
             rows = slice(r * P, (r + 1) * P)
             wide = slice(chunk_gate0[c] % HID, chunk_gate0[c] % HID + CHUNK)
             is_m = i < m_banks
-            last = i == len(banks) - 1
             res = m_sb if is_m else z_sb
             nc.vector.tensor_add(out=res[:, r, cols], in0=acc[:], in1=(bias_m if is_m else bias_z)[:, cols])
             if 4 <= i < 4 + m_banks:
@@ -205,35 +204,81 @@ def tile_koslmcell_pa_kernel(
                 if nt == N_TILES - 1:
                     nc.sync.dma_start(out=out_1[rows, wide], in_=m_sb[:, r, wide])
                 return
-            adder = nc.vector if last else nc.gpsimd
-            adder.tensor_add(out=innov_sb[:, r, cols], in0=innov_sb[:, r, cols], in1=z_sb[:, r, cols])
-            if c == chunks - 1 and r == ROW_TILES - 1:
-                nc.sync.dma_start(out=out_0[rows, cols], in_=z_sb[:, r, cols])
-                nc.sync.dma_start(out=out_2[rows, cols], in_=innov_sb[:, r, cols])
-            elif nt == N_TILES - 1:
-                nc.sync.dma_start(out=out_0[rows, wide], in_=z_sb[:, r, wide])
-                nc.sync.dma_start(out=out_2[rows, wide], in_=innov_sb[:, r, wide])
+            if i % 2 == 0:
+                last_sum(nc.gpsimd, i, cols)
+                if i > m_banks:
+                    c1, r1, nt1 = banks[i - 1]
+                    last_sum(nc.vector, i - 1, out_cols(c1, nt1))
+                    store_z(i - 1, slice(chunk_gate0[c1] % HID, chunk_gate0[c1] % HID + CHUNK))
 
-        for c in range(2):
+        tiles_of_half = HID // N_TILE
+        flip(0, 0)
+        flip(0, 1)
+        quantise(0)
+        load_chunk(1)
+        nc.sync.dma_start(out=c_sb[:], in_=c_prev.rearrange("(r p) n -> p r n", p=P))
+        for t in range(tiles_of_half):
+            bank = spread(tiles_of_half + t)
+            nc.scalar.copy(out=bias_m[:, t * N_TILE : (t + 1) * N_TILE], in_=bank[:])
+        for t in range(tiles_of_half):
+            bank = spread(GATES // N_TILE + t)
+            nc.scalar.activation(out=decay[:, t * N_TILE : (t + 1) * N_TILE], in_=bank[:], func=ACT.Exp)
+        for c in range(chunks):
+            x_first = c < chunks - 1
             accs = []
-            for b in range(len(banks_of_chunk)):
-                acc = psum.tile([P, N_TILE], F32, tag="bank")
-                accs.append(acc)
-            for g in range(2):
-                for b, (r, nt) in enumerate(banks_of_chunk):
-                    mx_pass(accs[b], c, r, nt, g)
-            for b, (r, nt) in enumerate(banks_of_chunk):
-                for g in range(2, PASSES):
-                    mx_pass(accs[b], c, r, nt, g)
-                finish(c * len(banks_of_chunk) + b, accs[b])
+            if x_first:
+                for b in range(len(banks_of_chunk)):
+                    acc = psum.tile([P, N_TILE], F32, tag="bank")
+                    accs.append(acc)
+                for g in range(X_PASSES):
+                    for b, (r, nt) in enumerate(banks_of_chunk):
+                        mx_pass(accs[b], c, r, nt, g)
             if c == 0:
-                z_banks = [spread(vec_z, n0) for n0 in range(0, HID, N_TILE)]
-                for n, bank in enumerate(z_banks):
-                    nc.scalar.copy(out=bias_z[:, n * N_TILE : (n + 1) * N_TILE], in_=bank[:])
-
-        for c in range(2, chunks):
+                flip(1, 0)
+                flip(1, 1)
+                flip(2, 0)
+                flip(2, 1)
+                quantise(1)
+                quantise(2)
+                for t in range(tiles_of_half):
+                    spread_bias(bias_z, 0, t)
+                load_chunk(2)
+                load_chunk(3)
             for b, (r, nt) in enumerate(banks_of_chunk):
-                acc = psum.tile([P, N_TILE], F32, tag="bank")
-                for g in range(PASSES):
-                    mx_pass(acc, c, r, nt, g)
-                finish(c * len(banks_of_chunk) + b, acc)
+                i = c * len(banks_of_chunk) + b
+                if i < len(banks) - 1:
+                    if x_first:
+                        acc = accs[b]
+                    else:
+                        acc = psum.tile([P, N_TILE], F32, tag="bank")
+                    for g in range(X_PASSES if x_first else 0, PASSES):
+                        mx_pass(acc, c, r, nt, g)
+                    finish(i, acc)
+
+        i = len(banks) - 1
+        c, r, nt = banks[i]
+        store_z(i - 1, out_cols(c, nt - 1))
+        before = None
+        for n0 in range(0, N_TILE, NARROW):
+            lo = nt * N_TILE + n0
+            cols = slice(chunk_gate0[c] % HID + lo, chunk_gate0[c] % HID + lo + NARROW)
+            acc = psum.tile([P, NARROW], F32, tag="bank")
+            for g in range(PASSES):
+                s = 0 if g < X_PASSES else 1
+                nc.tensor.matmul_mx(
+                    out=acc[:],
+                    lhsT=a_codes[g // 2][:, r, g % 2, :].bitcast(FP8X4),
+                    lhsT_scale=a_scales[g // 2][:, r, g % 2, :],
+                    rhs=w_words[c][s][:, g - s * X_PASSES, 2 * lo : 2 * (lo + NARROW)].bitcast(FP4X4),
+                    rhs_scale=w_scales[c][s][:, g - s * X_PASSES, lo : lo + NARROW],
+                    start=(g == 0),
+                    stop=(g == PASSES - 1),
+                )
+            nc.vector.tensor_add(out=z_sb[:, r, cols], in0=acc[:], in1=bias_z[:, cols])
+            nc.scalar.activation(out=z_sb[:, r, cols], in_=z_sb[:, r, cols], func=ACT.Tanh)
+            if before is not None:
+                last_sum(nc.vector, i, before)
+                store_z(i, before)
+            before = cols
+        last_sum(nc.vector, i, before)
+        store_z(i, before)

@@ -105,8 +105,8 @@ def tile_koslmcell_pa_kernel(
         for row0, vec in ((0, b_ih), (8, b_hh), (16, z_bias), (20, m_bias), (24, log_lambda)):
             by_tile = vec.rearrange("(j n) -> j n", n=N_TILE)
             nc.sync.dma_start(out=vec_rows[row0 : row0 + by_tile.shape[0], :], in_=by_tile)
-        load_scales(0, 0)
         load_words(0, 0)
+        load_scales(0, 0)
         nc.sync.dma_start(out=h_sb[:], in_=h_prev.rearrange("(r p) k -> p r k", p=P))
         load_scales(0, 1)
         load_words(0, 1)
@@ -116,7 +116,6 @@ def tile_koslmcell_pa_kernel(
                 nc.vector.memset(w_scales[c][s][:].rearrange("p g n -> p (g n)").bitcast(I32), 0)
             for s in range(2):
                 load_scales(c, s)
-            for s in range(2):
                 load_words(c, s)
 
         def flip(i, r):
@@ -201,8 +200,8 @@ def tile_koslmcell_pa_kernel(
             if is_m:
                 nc.scalar.mul(m_sb[:, r, cols], m_sb[:, r, cols], M_SCALE)
                 nc.gpsimd.tensor_mul(innov_sb[:, r, cols], m_sb[:, r, cols], decay[:, cols])
-                if nt == N_TILES - 1:
-                    nc.sync.dma_start(out=out_1[rows, wide], in_=m_sb[:, r, wide])
+                if c == 1 and nt == N_TILES - 1:
+                    nc.sync.dma_start(out=out_1[rows, :], in_=m_sb[:, r, :])
                 return
             if i % 2 == 0:
                 last_sum(nc.gpsimd, i, cols)

@@ -105,18 +105,17 @@ def tile_koslmcell_pa_kernel(
         for row0, vec in ((0, b_ih), (8, b_hh), (16, z_bias), (20, m_bias), (24, log_lambda)):
             by_tile = vec.rearrange("(j n) -> j n", n=N_TILE)
             nc.sync.dma_start(out=vec_rows[row0 : row0 + by_tile.shape[0], :], in_=by_tile)
-        load_words(0, 0)
-        load_scales(0, 0)
         nc.sync.dma_start(out=h_sb[:], in_=h_prev.rearrange("(r p) k -> p r k", p=P))
-        load_scales(0, 1)
-        load_words(0, 1)
+        for s in range(2):
+            load_words(0, s)
+            load_scales(0, s)
 
         def load_chunk(c):
             for s in range(2):
                 nc.vector.memset(w_scales[c][s][:].rearrange("p g n -> p (g n)").bitcast(I32), 0)
             for s in range(2):
-                load_scales(c, s)
                 load_words(c, s)
+                load_scales(c, s)
 
         def flip(i, r):
             base = 0 if i == 0 else (i - 1) * K_PASS
@@ -222,6 +221,16 @@ def tile_koslmcell_pa_kernel(
         for t in range(tiles_of_half):
             bank = spread(GATES // N_TILE + t)
             nc.scalar.activation(out=decay[:, t * N_TILE : (t + 1) * N_TILE], in_=bank[:], func=ACT.Exp)
+        flip(1, 0)
+        flip(1, 1)
+        flip(2, 0)
+        flip(2, 1)
+        quantise(1)
+        quantise(2)
+        for t in range(tiles_of_half):
+            spread_bias(bias_z, 0, t)
+        load_chunk(2)
+        load_chunk(3)
         for c in range(chunks):
             x_first = c < chunks - 1
             accs = []
@@ -232,17 +241,6 @@ def tile_koslmcell_pa_kernel(
                 for g in range(X_PASSES):
                     for b, (r, nt) in enumerate(banks_of_chunk):
                         mx_pass(accs[b], c, r, nt, g)
-            if c == 0:
-                flip(1, 0)
-                flip(1, 1)
-                flip(2, 0)
-                flip(2, 1)
-                quantise(1)
-                quantise(2)
-                for t in range(tiles_of_half):
-                    spread_bias(bias_z, 0, t)
-                load_chunk(2)
-                load_chunk(3)
             for b, (r, nt) in enumerate(banks_of_chunk):
                 i = c * len(banks_of_chunk) + b
                 if i < len(banks) - 1:

from contextlib import ExitStack

import concourse.mybir as mybir
from concourse.masks import make_identity

F32 = mybir.dt.float32
BF16 = mybir.dt.bfloat16
I32 = mybir.dt.int32
U32 = mybir.dt.uint32
U8 = mybir.dt.uint8
FP8X4 = mybir.dt.float8_e4m3fn_x4
FP4X4 = mybir.dt.float4_e2m1fn_x4
ACT = mybir.ActivationFunctionType

P = 128
K_PASS = 512
BATCH, D_IN, HID = 256, 1024, 2048
GATES = 2 * HID
K_ALL = D_IN + HID
PASSES = K_ALL // K_PASS
X_PASSES = D_IN // K_PASS
PAIRS = PASSES // 2
ROW_TILES = BATCH // P
N_TILE = 512
CHUNK = 1024
N_TILES = CHUNK // N_TILE
NARROW = 128
M_SCALE = 1.5

FLOPS = 2 * BATCH * K_ALL * GATES


def tile_koslmcell_pa_kernel(
    tc, x, h_prev, c_prev, W_ih_words, W_ih_scales, b_ih, W_hh_words, W_hh_scales, b_hh,
    log_lambda, z_bias, m_bias, out_0, out_1, out_2,
):
    nc = tc.nc
    with ExitStack() as ctx:
        keep = ctx.enter_context(tc.tile_pool(name="keep", bufs=1))
        psum = ctx.enter_context(tc.psum_pool(name="psum", bufs=8))
        ctx.enter_context(tc.manual_schedule())

        chunk_gate0 = [HID, HID + CHUNK, 0, CHUNK]
        chunks = len(chunk_gate0)

        x_sb = [keep.tile([P, D_IN], BF16, name="x_sb%d" % r) for r in range(ROW_TILES)]
        h_sb = keep.tile([P, ROW_TILES, HID], BF16)
        c_sb = keep.tile([P, ROW_TILES, HID], BF16)
        grouped = [
            keep.tile([P, ROW_TILES, 2, K_PASS], BF16, align_bytes=64, name="grouped%d" % i) for i in range(PAIRS)
        ]
        a_codes = [keep.tile([P, ROW_TILES, 2, P], U32, align_bytes=64, name="a_codes%d" % i) for i in range(PAIRS)]
        a_scales = [keep.tile([P, ROW_TILES, 2, P], U8, align_bytes=64, name="a_scales%d" % i) for i in range(PAIRS)]
        w_passes = (X_PASSES, PASSES - X_PASSES)
        w_words = [
            [keep.tile([P, w_passes[s], 2 * CHUNK], U8, align_bytes=64, name="w_words%d_%d" % (c, s)) for s in range(2)]
            for c in range(chunks)
        ]
        w_scales = [
            [keep.tile([P, w_passes[s], CHUNK], U8, align_bytes=64, name="w_scales%d_%d" % (c, s)) for s in range(2)]
            for c in range(chunks)
        ]
        vec_rows = keep.tile([P, N_TILE], BF16)
        pick = keep.tile([P, 12], BF16)
        pick_sum = keep.tile([P, 8], F32)
        ident = keep.tile([P, P], F32)
        warm = keep.tile([P, 1], F32)
        bias_m = keep.tile([P, HID], F32)
        bias_z = keep.tile([P, HID], F32)
        decay = keep.tile([P, HID], F32)
        z_sb = keep.tile([P, ROW_TILES, HID], F32)
        m_sb = keep.tile([P, ROW_TILES, HID], F32)
        innov_sb = keep.tile([P, ROW_TILES, HID], F32)

        nc.vector.memset(vec_rows[:].bitcast(I32), 0)
        make_identity(nc, ident[:])
        nc.gpsimd.memset(warm[:], 0.0)
        nc.scalar.activation(out=warm[:], in_=warm[:], func=ACT.Exp)
        nc.vector.memset(w_scales[0][0][:].rearrange("p g n -> p (g n)").bitcast(I32), 0)
        nc.vector.tensor_add(out=pick_sum[:], in0=ident[:, 0:8], in1=ident[:, 8:16])
        nc.vector.tensor_add(out=pick[:, 0:8], in0=pick_sum[:], in1=ident[:, 16:24])
        nc.vector.tensor_copy(out=pick[:, 8:12], in_=ident[:, 24:28])
        nc.vector.memset(w_scales[0][1][:].rearrange("p g n -> p (g n)").bitcast(I32), 0)

        def load_scales(c, s):
            col0 = chunk_gate0[c]
            by_row = (W_ih_scales, W_hh_scales)[s].bitcast(I32).rearrange("g (q j) w -> j q g w", j=4)
            for j in range(4):
                nc.sync.dma_start(
                    out=w_scales[c][s][j:P:32, :, :].bitcast(I32),
                    in_=by_row[j, :, :, col0 // 4 : (col0 + CHUNK) // 4],
                )

        def load_words(c, s):
            col0 = chunk_gate0[c]
            nc.sync.dma_start(
                out=w_words[c][s][:].bitcast(I32),
                in_=(W_ih_words, W_hh_words)[s].bitcast(I32).rearrange("g p w -> p g w")[
                    :, :, col0 // 2 : (col0 + CHUNK) // 2
                ],
            )

        for r in range(ROW_TILES):
            nc.sync.dma_start(out=x_sb[r][:], in_=x[r * P : (r + 1) * P, :])
        for row0, vec in ((0, b_ih), (8, b_hh), (16, z_bias), (20, m_bias), (24, log_lambda)):
            by_tile = vec.rearrange("(j n) -> j n", n=N_TILE)
            nc.sync.dma_start(out=vec_rows[row0 : row0 + by_tile.shape[0], :], in_=by_tile)
        nc.sync.dma_start(out=h_sb[:], in_=h_prev.rearrange("(r p) k -> p r k", p=P))
        for s in range(2):
            load_words(0, s)
            load_scales(0, s)

        def load_chunk(c):
            for s in range(2):
                nc.vector.memset(w_scales[c][s][:].rearrange("p g n -> p (g n)").bitcast(I32), 0)
            for s in range(2):
                load_words(c, s)
                load_scales(c, s)

        def flip(i, r):
            base = 0 if i == 0 else (i - 1) * K_PASS
            src_words = (x_sb[r][:] if i == 0 else h_sb[:, r, :]).bitcast(F32)
            flipped = psum.tile([P, 2, 2, P], F32, tag="bank")
            for gg in range(2):
                for u in range(2):
                    w0 = base + gg * (K_PASS // 2)
                    nc.tensor.transpose(flipped[:, gg, u, :], src_words[:, w0 + u : w0 + K_PASS // 2 : 2], ident[:])
            side_by_side = grouped[i][:, r, :, :].bitcast(F32).rearrange("p g (b u) -> p g b u", u=2)
            if r == 0:
                nc.vector.tensor_copy(out=side_by_side, in_=flipped[:].rearrange("p g u b -> p g b u"))
            else:
                nc.scalar.copy(out=side_by_side, in_=flipped[:].rearrange("p g u b -> p g b u"))

        def quantise(i):
            nc.vector.quantize_mx(
                out=a_codes[i][:].rearrange("p r g b -> p (r g b)").bitcast(FP8X4),
                scales=a_scales[i][:].rearrange("p r g b -> p (r g b)"),
                in_=grouped[i][:].rearrange("p r g k -> p (r g k)"),
            )

        def spread(j):
            bank = psum.tile([P, N_TILE], F32, tag="bank")
            nc.tensor.matmul(
                bank[:], lhsT=pick[:, j : j + 1].to_broadcast([P, P]), rhs=vec_rows[:], start=True, stop=True
            )
            return bank

        def spread_bias(bias, j0, t):
            bank = spread(j0 + t)
            if t % 2 == 0:
                nc.vector.tensor_copy(out=bias[:, t * N_TILE : (t + 1) * N_TILE], in_=bank[:])
            else:
                nc.scalar.copy(out=bias[:, t * N_TILE : (t + 1) * N_TILE], in_=bank[:])

        def mx_pass(acc, c, r, nt, g):
            s = 0 if g < X_PASSES else 1
            g_local = g - s * X_PASSES
            nc.tensor.matmul_mx(
                out=acc[:],
                lhsT=a_codes[g // 2][:, r, g % 2, :].bitcast(FP8X4),
                lhsT_scale=a_scales[g // 2][:, r, g % 2, :],
                rhs=w_words[c][s][:, g_local, 2 * nt * N_TILE : 2 * (nt + 1) * N_TILE].bitcast(FP4X4),
                rhs_scale=w_scales[c][s][:, g_local, nt * N_TILE : (nt + 1) * N_TILE],
                start=(g == 0),
                stop=(g == PASSES - 1),
            )

        banks_of_chunk = [(r, nt) for r in range(ROW_TILES) for nt in range(N_TILES)]
        banks = [(c, r, nt) for c in range(chunks) for r, nt in banks_of_chunk]
        m_banks = len(banks) // 2

        def out_cols(c, nt):
            col0 = chunk_gate0[c] % HID + nt * N_TILE
            return slice(col0, col0 + N_TILE)

        def last_sum(engine, i, cols):
            c, r, nt = banks[i]
            engine.tensor_add(out=innov_sb[:, r, cols], in0=innov_sb[:, r, cols], in1=z_sb[:, r, cols])

        def store_z(i, cols):
            c, r, nt = banks[i]
            rows = slice(r * P, (r + 1) * P)
            nc.sync.dma_start(out=out_0[rows, cols], in_=z_sb[:, r, cols])
            nc.sync.dma_start(out=out_2[rows, cols], in_=innov_sb[:, r, cols])

        def finish(i, acc):
            c, r, nt = banks[i]
            cols = out_cols(c, nt)
            rows = slice(r * P, (r + 1) * P)
            wide = slice(chunk_gate0[c] % HID, chunk_gate0[c] % HID + CHUNK)
            is_m = i < m_banks
            res = m_sb if is_m else z_sb
            nc.vector.tensor_add(out=res[:, r, cols], in0=acc[:], in1=(bias_m if is_m else bias_z)[:, cols])
            if 4 <= i < 4 + m_banks:
                c4, r4, nt4 = banks[i - 4]
                cols4 = out_cols(c4, nt4)
                nc.vector.tensor_mul(innov_sb[:, r4, cols4], innov_sb[:, r4, cols4], c_sb[:, r4, cols4])
            nc.scalar.activation(out=res[:, r, cols], in_=res[:, r, cols], func=ACT.Tanh)
            if is_m:
                nc.scalar.mul(m_sb[:, r, cols], m_sb[:, r, cols], M_SCALE)
                nc.gpsimd.tensor_mul(innov_sb[:, r, cols], m_sb[:, r, cols], decay[:, cols])
                if c == 1 and nt == N_TILES - 1:
                    nc.sync.dma_start(out=out_1[rows, :], in_=m_sb[:, r, :])
                return
            if i % 2 == 0:
                last_sum(nc.gpsimd, i, cols)
                if i > m_banks:
                    c1, r1, nt1 = banks[i - 1]
                    last_sum(nc.vector, i - 1, out_cols(c1, nt1))
                    store_z(i - 1, slice(chunk_gate0[c1] % HID, chunk_gate0[c1] % HID + CHUNK))

        tiles_of_half = HID // N_TILE
        flip(0, 0)
        flip(0, 1)
        quantise(0)
        load_chunk(1)
        nc.sync.dma_start(out=c_sb[:], in_=c_prev.rearrange("(r p) n -> p r n", p=P))
        for t in range(tiles_of_half):
            bank = spread(tiles_of_half + t)
            nc.scalar.copy(out=bias_m[:, t * N_TILE : (t + 1) * N_TILE], in_=bank[:])
        for t in range(tiles_of_half):
            bank = spread(GATES // N_TILE + t)
            nc.scalar.activation(out=decay[:, t * N_TILE : (t + 1) * N_TILE], in_=bank[:], func=ACT.Exp)
        flip(1, 0)
        flip(1, 1)
        flip(2, 0)
        flip(2, 1)
        quantise(1)
        quantise(2)
        for t in range(tiles_of_half):
            spread_bias(bias_z, 0, t)
        load_chunk(2)
        load_chunk(3)
        for c in range(chunks):
            x_first = c < chunks - 1
            accs = []
            if x_first:
                for b in range(len(banks_of_chunk)):
                    acc = psum.tile([P, N_TILE], F32, tag="bank")
                    accs.append(acc)
                for g in range(X_PASSES):
                    for b, (r, nt) in enumerate(banks_of_chunk):
                        mx_pass(accs[b], c, r, nt, g)
            for b, (r, nt) in enumerate(banks_of_chunk):
                i = c * len(banks_of_chunk) + b
                if i < len(banks) - 1:
                    if x_first:
                        acc = accs[b]
                    else:
                        acc = psum.tile([P, N_TILE], F32, tag="bank")
                    for g in range(X_PASSES if x_first else 0, PASSES):
                        mx_pass(acc, c, r, nt, g)
                    finish(i, acc)

        i = len(banks) - 1
        c, r, nt = banks[i]
        store_z(i - 1, out_cols(c, nt - 1))
        before = None
        for n0 in range(0, N_TILE, NARROW):
            lo = nt * N_TILE + n0
            cols = slice(chunk_gate0[c] % HID + lo, chunk_gate0[c] % HID + lo + NARROW)
            acc = psum.tile([P, NARROW], F32, tag="bank")
            for g in range(PASSES):
                s = 0 if g < X_PASSES else 1
                nc.tensor.matmul_mx(
                    out=acc[:],
                    lhsT=a_codes[g // 2][:, r, g % 2, :].bitcast(FP8X4),
                    lhsT_scale=a_scales[g // 2][:, r, g % 2, :],
                    rhs=w_words[c][s][:, g - s * X_PASSES, 2 * lo : 2 * (lo + NARROW)].bitcast(FP4X4),
                    rhs_scale=w_scales[c][s][:, g - s * X_PASSES, lo : lo + NARROW],
                    start=(g == 0),
                    stop=(g == PASSES - 1),
                )
            nc.vector.tensor_add(out=z_sb[:, r, cols], in0=acc[:], in1=bias_z[:, cols])
            nc.scalar.activation(out=z_sb[:, r, cols], in_=z_sb[:, r, cols], func=ACT.Tanh)
            if before is not None:
                last_sum(nc.vector, i, before)
                store_z(i, before)
            before = cols
        last_sum(nc.vector, i, before)
        store_z(i, before)
